import numpy as np
import ml_dtypes


def mxq(x, axis, fmt="e4m3"):
    dtype, down = {"e4m3": (ml_dtypes.float8_e4m3fn, 7), "e5m2": (ml_dtypes.float8_e5m2, 14)}[fmt]
    v = np.moveaxis(np.asarray(x, np.float32).astype(ml_dtypes.bfloat16).astype(np.float64), axis, -1)
    blocks = v.reshape(v.shape[:-1] + (-1, 32))
    amax = np.abs(blocks).max(-1, keepdims=True)
    byte = np.maximum(np.where(amax > 0, np.frexp(amax)[1] - 1 + 127, 0) - down, 1)
    scale = np.exp2(byte - 127.0)
    codes = (blocks / scale).astype(np.float32).astype(dtype).astype(np.float64)
    return np.moveaxis((codes * scale).reshape(v.shape), -1, axis)


BF16 = ml_dtypes.bfloat16


def bf(x):
    return np.asarray(x, np.float32).astype(BF16)


def f64(x):
    return np.asarray(x).astype(np.float64)


C, H, N, L = 1, 512, 512, 8192


def setup_inputs():
    return {"W": bf(np.random.standard_normal((C, H, N)) / np.sqrt(N)), "Lambda_im": bf(np.random.uniform(0.0, 2.0 * np.pi, N)), "L": L}


def reference(W, Lambda_im, L):
    pos = np.arange(L, dtype=np.float64)
    S = np.cos(f64(Lambda_im)[:, None] * pos[None, :])
    return mxq(f64(W), 2, "e4m3") @ mxq(S, 0, "e4m3")

@@ -1,0 +1,230 @@
+import math
+
+import concourse.mybir as mybir
+from concourse.masks import make_identity
+
+F32 = mybir.dt.float32
+BF16 = mybir.dt.bfloat16
+I32 = mybir.dt.int32
+U32 = mybir.dt.uint32
+U8 = mybir.dt.uint8
+FP8X4 = mybir.dt.float8_e4m3fn_x4
+ALU = mybir.AluOpType
+ACT = mybir.ActivationFunctionType
+
+P = 128
+PACK = 4
+BLOCK = 512
+SUPER = 512
+T_GROUP = 1
+
+FLOPS = 2 * 512 * 512 * 8192
+
+TWO_PI_HI = 3217.0 / 512.0
+TWO_PI_LO = 2.0 * math.pi - TWO_PI_HI
+ROUND_SHIFT = -0.125
+
+
+def tile_dlrkernel_t_kernel(tc, W, Lambda_im, L, out):
+    nc = tc.nc
+    H = W.shape[1]
+    N = W.shape[2]
+    assert N == P * PACK and H % (2 * P) == 0 and L % (2 * SUPER) == 0
+    h_tiles = H // P
+    subs = SUPER // BLOCK
+    pairs = L // (2 * BLOCK)
+    supers = L // (2 * SUPER)
+    centre = (L - BLOCK) // 2
+    width = BLOCK + pairs
+    out_view = out[0].rearrange("(a p) l -> p a l", p=P)
+
+    with tc.tile_pool(name="const", bufs=1) as const, tc.tile_pool(name="work", bufs=3) as work, tc.psum_pool(
+        name="psum", bufs=8
+    ) as psum, tc.manual_schedule():
+        lam_bf = const.tile([P, PACK], BF16)
+        nc.sync.dma_start(out=lam_bf[:], in_=Lambda_im.rearrange("(p t) -> p t", t=PACK))
+        w_sb = const.tile([P, h_tiles, N], BF16)
+        nc.sync.dma_start(out=w_sb[:], in_=W[0].rearrange("(a p) n -> p a n", p=P))
+
+        warm = const.tile([P, 1], F32)
+        nc.vector.memset(warm[:], 0.0)
+        nc.scalar.activation(out=warm[:], in_=warm[:], func=ACT.Sin)
+
+        pos = const.tile([P, width], F32)
+        nc.gpsimd.iota(
+            pos[:, 0:BLOCK], pattern=[[1, BLOCK]], base=centre, channel_multiplier=0, allow_small_or_imprecise_dtypes=True
+        )
+        nc.gpsimd.iota(
+            pos[:, BLOCK:width],
+            pattern=[[BLOCK, pairs]],
+            base=BLOCK // 2,
+            channel_multiplier=0,
+            allow_small_or_imprecise_dtypes=True,
+        )
+        ident = const.tile([P, P], F32)
+        make_identity(nc, ident[:])
+
+        lam = const.tile([P, PACK], F32)
+        nc.vector.tensor_copy(out=lam[:], in_=lam_bf[:])
+        turns = const.tile([P, PACK], F32)
+        nc.vector.tensor_scalar(out=turns[:], in0=lam[:], scalar1=1.0 / (2.0 * math.pi), scalar2=None, op0=ALU.mult)
+
+        w_grouped = const.tile([P, H, 2], F32, align_bytes=64)
+        w_codes = const.tile([P, H], U32, align_bytes=64)
+        w_scales = const.tile([P, H], U8, align_bytes=64)
+        turned_tiles = []
+        for half in range(h_tiles // 2):
+            turned = psum.tile([P, 2, 2, P], F32, name="turned", tag="acc")
+            turned_tiles.append(turned)
+            for a in range(2):
+                words = w_sb[:, 2 * half + a, :].bitcast(F32).rearrange("p (q u) -> p u q", u=2)
+                for u in range(2):
+                    nc.tensor.transpose(turned[:, a, u, :], words[:, u, :], ident[:])
+
+        def w_copies():
+            for half in range(h_tiles // 2):
+                nc.scalar.copy(
+                    out=w_grouped[:, 2 * P * half : 2 * P * (half + 1), :].rearrange("p (a h) u -> p a h u", a=2),
+                    in_=turned_tiles[half][:].rearrange("p a u h -> p a h u"),
+                )
+
+        def w_quantise():
+            nc.vector.quantize_mx(
+                out=w_codes[:].bitcast(FP8X4),
+                scales=w_scales[:],
+                in_=w_grouped[:].rearrange("p h u -> p (h u)").bitcast(BF16),
+            )
+
+        table = const.tile([P, PACK, 2, width], F32)
+        k_int = const.tile([P, PACK, width], I32)
+        angle = const.tile([P, PACK, width], F32)
+        part = const.tile([P, PACK, width], F32)
+        red = const.tile([P, PACK, width], F32)
+        fold = const.tile([P, PACK, 2, width], F32)
+
+        u_tiles = {}
+        v_tiles = {}
+
+        def product_list(m):
+            return [(r, t) for t in range(PACK) for r in range(subs)]
+
+        def new_products(m):
+            u_tiles[m] = work.tile([P, PACK, SUPER], F32, name="u_t", tag="u_t")
+            v_tiles[m] = work.tile([P, PACK, SUPER], F32, name="v_t", tag="v_t")
+
+        def product(m, r, t, which, engine):
+            k = subs * m + r
+            dst = (u_tiles[m] if which == 0 else v_tiles[m])[:, t, r * BLOCK : (r + 1) * BLOCK]
+            src = table[:, t, which, 0:BLOCK]
+            factor = table[:, t, which, BLOCK + k : BLOCK + k + 1]
+            if engine == "v":
+                nc.vector.tensor_scalar(out=dst, in0=src, scalar1=factor, scalar2=None, op0=ALU.mult)
+            else:
+                nc.scalar.activation(out=dst, in_=src, func=ACT.Copy, scale=factor)
+
+        new_products(0)
+        groups = [list(range(g, g + T_GROUP)) for g in range(0, PACK, T_GROUP)]
+        for gi, ts in enumerate(groups):
+            lo, hi = ts[0], ts[-1] + 1
+            for t in ts:
+                nc.vector.tensor_scalar(
+                    out=k_int[:, t, :], in0=pos[:], scalar1=turns[:, t : t + 1], scalar2=ROUND_SHIFT, op0=ALU.mult, op1=ALU.add
+                )
+                nc.vector.tensor_scalar(out=angle[:, t, :], in0=pos[:], scalar1=lam[:, t : t + 1], scalar2=None, op0=ALU.mult)
+            nc.vector.scalar_tensor_tensor(
+                out=part[:, lo:hi, :], in0=k_int[:, lo:hi, :], scalar=-TWO_PI_HI, in1=angle[:, lo:hi, :], op0=ALU.mult, op1=ALU.add
+            )
+            nc.vector.scalar_tensor_tensor(
+                out=red[:, lo:hi, :], in0=k_int[:, lo:hi, :], scalar=-TWO_PI_LO, in1=part[:, lo:hi, :], op0=ALU.mult, op1=ALU.add
+            )
+            nc.scalar.activation(out=fold[:, lo:hi, 0, :], in_=red[:, lo:hi, :], func=ACT.Abs)
+            nc.scalar.activation(out=fold[:, lo:hi, 1, :], in_=red[:, lo:hi, :], func=ACT.Abs, bias=-0.5 * math.pi)
+            nc.scalar.activation(
+                out=table[:, lo:hi, :, :], in_=fold[:, lo:hi, :, :], func=ACT.Sin, scale=-1.0, bias=0.5 * math.pi
+            )
+            if gi == 1:
+                w_copies()
+        w_quantise()
+        for r, t in product_list(0):
+            product(0, r, t, 0, "v")
+            product(0, r, t, 1, "v")
+
+        grouped_tiles = {}
+        code_tiles = {}
+        acc_tiles = {}
+
+        def combine(m, s):
+            grouped = work.tile([P, SUPER, PACK], BF16, name="grouped", tag="grouped", align_bytes=64)
+            grouped_tiles[(m, s)] = grouped
+            if s == 0:
+                spans = [(0, 0, SUPER)]
+            else:
+                spans = [((subs - 1 - r) * BLOCK, r * BLOCK, BLOCK) for r in range(subs)]
+            for dst0, src0, n in spans:
+                nc.vector.tensor_tensor(
+                    out=grouped[:, dst0 : dst0 + n, :].rearrange("p (c i) t -> p c t i", i=4),
+                    in0=u_tiles[m][:, :, src0 : src0 + n].rearrange("p t (c i) -> p c t i", i=4),
+                    in1=v_tiles[m][:, :, src0 : src0 + n].rearrange("p t (c i) -> p c t i", i=4),
+                    op=ALU.subtract if s == 0 else ALU.add,
+                )
+
+        def quantise(m, s):
+            codes = work.tile([P, SUPER], U32, name="codes", tag="codes", align_bytes=64)
+            scales = work.tile([P, SUPER], U8, name="scales", tag="scales", align_bytes=64)
+            code_tiles[(m, s)] = (codes, scales)
+            nc.vector.quantize_mx(
+                out=codes[:].bitcast(FP8X4), scales=scales[:], in_=grouped_tiles[(m, s)][:].rearrange("p l t -> p (l t)")
+            )
+
+        def multiply(m, s):
+            codes, scales = code_tiles[(m, s)]
+            acc_tiles[(m, s)] = []
+            for a in range(h_tiles):
+                acc = psum.tile([P, SUPER], F32, name="acc", tag="acc")
+                acc_tiles[(m, s)].append(acc)
+                nc.tensor.matmul_mx(
+                    out=acc[:],
+                    lhsT=w_codes[:, a * P : (a + 1) * P].bitcast(FP8X4),
+                    lhsT_scale=w_scales[:, a * P : (a + 1) * P],
+                    rhs=codes[:].bitcast(FP8X4),
+                    rhs_scale=scales[:],
+                    start=True,
+                    stop=True,
+                )
+
+        def evacuate(m, s, engines, split):
+            start = L // 2 + SUPER * m if s == 0 else L // 2 - SUPER * (m + 1)
+            stage = work.tile([P, h_tiles, SUPER], F32, name="stage", tag="stage", bufs=4)
+            for a in range(h_tiles):
+                if engines[a] == "v":
+                    nc.vector.tensor_copy(out=stage[:, a, :], in_=acc_tiles[(m, s)][a][:])
+                else:
+                    nc.scalar.copy(out=stage[:, a, :], in_=acc_tiles[(m, s)][a][:])
+                if split:
+                    nc.sync.dma_start(out=out_view[:, a, start : start + SUPER], in_=stage[:, a, :])
+            if not split:
+                nc.sync.dma_start(out=out_view[:, :, start : start + SUPER], in_=stage[:])
+
+        vector_banks = []
+        for m in range(supers):
+            nxt = m + 1 < supers
+            todo = product_list(m + 1) if nxt else []
+            cut = len(todo) // 2
+            combine(m, 0)
+            if m > 0:
+                evacuate(m - 1, 1, "ssss", False)
+            if nxt:
+                new_products(m + 1)
+            for r, t in todo[:cut]:
+                product(m + 1, r, t, 0, "v")
+            quantise(m, 0)
+            multiply(m, 0)
+            for r, t in todo:
+                product(m + 1, r, t, 1, "s")
+            combine(m, 1)
+            for r, t in todo[cut:]:
+                product(m + 1, r, t, 0, "v")
+            quantise(m, 1)
+            multiply(m, 1)
+            evacuate(m, 0, "sssv" if m in vector_banks else "ssss", False)
+        evacuate(supers - 1, 1, "svsv", True)

@@ -14,7 +14,7 @@ ACT = mybir.ActivationFunctionType
 
 P = 128
 PACK = 4
-BLOCK = 512
+BLOCK = 256
 SUPER = 512
 T_GROUP = 1
 
@@ -142,9 +142,8 @@ def tile_dlrkernel_t_kernel(tc, W, Lambda_im, L, out):
             nc.scalar.activation(
                 out=table[:, lo:hi, :, :], in_=fold[:, lo:hi, :, :], func=ACT.Sin, scale=-1.0, bias=0.5 * math.pi
             )
-            if gi == 1:
+            if gi == 3:
                 w_copies()
-        w_quantise()
         for r, t in product_list(0):
             product(0, r, t, 0, "v")
             product(0, r, t, 1, "v")
@@ -153,13 +152,19 @@ def tile_dlrkernel_t_kernel(tc, W, Lambda_im, L, out):
         code_tiles = {}
         acc_tiles = {}
 
-        def combine(m, s):
-            grouped = work.tile([P, SUPER, PACK], BF16, name="grouped", tag="grouped", align_bytes=64)
-            grouped_tiles[(m, s)] = grouped
+        def spans_of(s):
             if s == 0:
-                spans = [(0, 0, SUPER)]
-            else:
-                spans = [((subs - 1 - r) * BLOCK, r * BLOCK, BLOCK) for r in range(subs)]
+                return [(0, 0, SUPER)]
+            return [((subs - 1 - r) * BLOCK, r * BLOCK, BLOCK) for r in range(subs)]
+
+        def new_block(m, s):
+            grouped_tiles[(m, s)] = work.tile([P, SUPER, PACK], BF16, name="grouped", tag="grouped", align_bytes=64)
+            codes = work.tile([P, SUPER], U32, name="codes", tag="codes", align_bytes=64)
+            scales = work.tile([P, SUPER], U8, name="scales", tag="scales", align_bytes=64)
+            code_tiles[(m, s)] = (codes, scales)
+
+        def combine(m, s, spans):
+            grouped = grouped_tiles[(m, s)]
             for dst0, src0, n in spans:
                 nc.vector.tensor_tensor(
                     out=grouped[:, dst0 : dst0 + n, :].rearrange("p (c i) t -> p c t i", i=4),
@@ -168,63 +173,81 @@ def tile_dlrkernel_t_kernel(tc, W, Lambda_im, L, out):
                     op=ALU.subtract if s == 0 else ALU.add,
                 )
 
-        def quantise(m, s):
-            codes = work.tile([P, SUPER], U32, name="codes", tag="codes", align_bytes=64)
-            scales = work.tile([P, SUPER], U8, name="scales", tag="scales", align_bytes=64)
-            code_tiles[(m, s)] = (codes, scales)
+        def quantise(m, s, c0, n):
+            codes, scales = code_tiles[(m, s)]
             nc.vector.quantize_mx(
-                out=codes[:].bitcast(FP8X4), scales=scales[:], in_=grouped_tiles[(m, s)][:].rearrange("p l t -> p (l t)")
+                out=codes[:, c0 : c0 + n].bitcast(FP8X4),
+                scales=scales[:, c0 : c0 + n],
+                in_=grouped_tiles[(m, s)][:, c0 : c0 + n, :].rearrange("p l t -> p (l t)"),
             )
 
-        def multiply(m, s):
+        def multiply(m, s, c0, n):
             codes, scales = code_tiles[(m, s)]
-            acc_tiles[(m, s)] = []
+            acc_tiles[(m, s, c0)] = []
             for a in range(h_tiles):
-                acc = psum.tile([P, SUPER], F32, name="acc", tag="acc")
-                acc_tiles[(m, s)].append(acc)
+                acc = psum.tile([P, n], F32, name="acc", tag="acc")
+                acc_tiles[(m, s, c0)].append(acc)
                 nc.tensor.matmul_mx(
                     out=acc[:],
                     lhsT=w_codes[:, a * P : (a + 1) * P].bitcast(FP8X4),
                     lhsT_scale=w_scales[:, a * P : (a + 1) * P],
-                    rhs=codes[:].bitcast(FP8X4),
-                    rhs_scale=scales[:],
+                    rhs=codes[:, c0 : c0 + n].bitcast(FP8X4),
+                    rhs_scale=scales[:, c0 : c0 + n],
                     start=True,
                     stop=True,
                 )
 
-        def evacuate(m, s, engines, split):
-            start = L // 2 + SUPER * m if s == 0 else L // 2 - SUPER * (m + 1)
-            stage = work.tile([P, h_tiles, SUPER], F32, name="stage", tag="stage", bufs=4)
+        def evacuate(m, s, c0, n, engines, split):
+            start = (L // 2 + SUPER * m if s == 0 else L // 2 - SUPER * (m + 1)) + c0
+            stage = work.tile([P, h_tiles, n], F32, name="stage", tag="stage", bufs=4)
             for a in range(h_tiles):
                 if engines[a] == "v":
-                    nc.vector.tensor_copy(out=stage[:, a, :], in_=acc_tiles[(m, s)][a][:])
+                    nc.vector.tensor_copy(out=stage[:, a, :], in_=acc_tiles[(m, s, c0)][a][:])
                 else:
-                    nc.scalar.copy(out=stage[:, a, :], in_=acc_tiles[(m, s)][a][:])
+                    nc.scalar.copy(out=stage[:, a, :], in_=acc_tiles[(m, s, c0)][a][:])
                 if split:
-                    nc.sync.dma_start(out=out_view[:, a, start : start + SUPER], in_=stage[:, a, :])
+                    nc.sync.dma_start(out=out_view[:, a, start : start + n], in_=stage[:, a, :])
             if not split:
-                nc.sync.dma_start(out=out_view[:, :, start : start + SUPER], in_=stage[:])
+                nc.sync.dma_start(out=out_view[:, :, start : start + n], in_=stage[:])
 
-        vector_banks = []
-        for m in range(supers):
-            nxt = m + 1 < supers
-            todo = product_list(m + 1) if nxt else []
+        last = supers - 1
+        for m in range(last):
+            todo = product_list(m + 1)
             cut = len(todo) // 2
-            combine(m, 0)
+            new_block(m, 0)
+            combine(m, 0, spans_of(0))
             if m > 0:
-                evacuate(m - 1, 1, "ssss", False)
-            if nxt:
-                new_products(m + 1)
+                evacuate(m - 1, 1, 0, SUPER, "ssss", False)
+            new_products(m + 1)
+            if m == 0:
+                w_quantise()
             for r, t in todo[:cut]:
                 product(m + 1, r, t, 0, "v")
-            quantise(m, 0)
-            multiply(m, 0)
+            quantise(m, 0, 0, SUPER)
+            multiply(m, 0, 0, SUPER)
             for r, t in todo:
                 product(m + 1, r, t, 1, "s")
-            combine(m, 1)
+            new_block(m, 1)
+            combine(m, 1, spans_of(1))
             for r, t in todo[cut:]:
                 product(m + 1, r, t, 0, "v")
-            quantise(m, 1)
-            multiply(m, 1)
-            evacuate(m, 0, "sssv" if m in vector_banks else "ssss", False)
-        evacuate(supers - 1, 1, "svsv", True)
+            quantise(m, 1, 0, SUPER)
+            multiply(m, 1, 0, SUPER)
+            evacuate(m, 0, 0, SUPER, "ssss", False)
+
+        pieces = spans_of(1)
+        new_block(last, 0)
+        combine(last, 0, spans_of(0))
+        evacuate(last - 1, 1, 0, SUPER, "ssss", False)
+        new_block(last, 1)
+        combine(last, 1, pieces[:1])
+        quantise(last, 0, 0, SUPER)
+        multiply(last, 0, 0, SUPER)
+        evacuate(last, 0, 0, SUPER, "ssss", False)
+        for i, (dst0, src0, n) in enumerate(pieces):
+            if i + 1 < len(pieces):
+                combine(last, 1, pieces[i + 1 : i + 2])
+            quantise(last, 1, dst0, n)
+            multiply(last, 1, dst0, n)
+        for i, (dst0, src0, n) in enumerate(pieces):
+            evacuate(last, 1, dst0, n, "svsv" if i + 1 == len(pieces) else "ssss", i + 1 == len(pieces))

@@ -17,6 +17,8 @@ PACK = 4
 BLOCK = 256
 SUPER = 512
 T_GROUP = 1
+FIRST_V_ON_VECTOR = 2
+U_ON_SCALAR = 1
 
 FLOPS = 2 * 512 * 512 * 8192
 
@@ -64,8 +66,7 @@ def tile_dlrkernel_t_kernel(tc, W, Lambda_im, L, out):
         ident = const.tile([P, P], F32)
         make_identity(nc, ident[:])
 
-        lam = const.tile([P, PACK], F32)
-        nc.vector.tensor_copy(out=lam[:], in_=lam_bf[:])
+        lam = lam_bf
         turns = const.tile([P, PACK], F32)
         nc.vector.tensor_scalar(out=turns[:], in0=lam[:], scalar1=1.0 / (2.0 * math.pi), scalar2=None, op0=ALU.mult)
 
@@ -142,11 +143,10 @@ def tile_dlrkernel_t_kernel(tc, W, Lambda_im, L, out):
             nc.scalar.activation(
                 out=table[:, lo:hi, :, :], in_=fold[:, lo:hi, :, :], func=ACT.Sin, scale=-1.0, bias=0.5 * math.pi
             )
-            if gi == 3:
-                w_copies()
         for r, t in product_list(0):
             product(0, r, t, 0, "v")
-            product(0, r, t, 1, "v")
+            product(0, r, t, 1, "v" if t < FIRST_V_ON_VECTOR else "s")
+        w_copies()
 
         grouped_tiles = {}
         code_tiles = {}
@@ -219,16 +219,23 @@ def tile_dlrkernel_t_kernel(tc, W, Lambda_im, L, out):
             if m > 0:
                 evacuate(m - 1, 1, 0, SUPER, "ssss", False)
             new_products(m + 1)
+            first = todo[U_ON_SCALAR:cut]
             if m == 0:
                 w_quantise()
-            for r, t in todo[:cut]:
+                first = []
+            for r, t in first:
                 product(m + 1, r, t, 0, "v")
             quantise(m, 0, 0, SUPER)
             multiply(m, 0, 0, SUPER)
+            for r, t in todo[:U_ON_SCALAR]:
+                product(m + 1, r, t, 0, "s")
             for r, t in todo:
                 product(m + 1, r, t, 1, "s")
             new_block(m, 1)
             combine(m, 1, spans_of(1))
+            if m == 0:
+                for r, t in todo[U_ON_SCALAR:cut]:
+                    product(m + 1, r, t, 0, "v")
             for r, t in todo[cut:]:
                 product(m + 1, r, t, 0, "v")
             quantise(m, 1, 0, SUPER)
@@ -250,4 +257,4 @@ def tile_dlrkernel_t_kernel(tc, W, Lambda_im, L, out):
             quantise(last, 1, dst0, n)
             multiply(last, 1, dst0, n)
         for i, (dst0, src0, n) in enumerate(pieces):
-            evacuate(last, 1, dst0, n, "svsv" if i + 1 == len(pieces) else "ssss", i + 1 == len(pieces))
+            evacuate(last, 1, dst0, n, "svsv", i + 1 == len(pieces))

@@ -42,7 +42,7 @@ def tile_dlrkernel_t_kernel(tc, W, Lambda_im, L, out):
 
     with tc.tile_pool(name="const", bufs=1) as const, tc.tile_pool(name="work", bufs=3) as work, tc.psum_pool(
         name="psum", bufs=8
-    ) as psum, tc.manual_schedule():
+    ) as psum:
         lam_bf = const.tile([P, PACK], BF16)
         nc.sync.dma_start(out=lam_bf[:], in_=Lambda_im.rearrange("(p t) -> p t", t=PACK))
         w_sb = const.tile([P, h_tiles, N], BF16)

@@ -245,16 +245,16 @@ def tile_dlrkernel_t_kernel(tc, W, Lambda_im, L, out):
         pieces = spans_of(1)
         new_block(last, 0)
         combine(last, 0, spans_of(0))
-        evacuate(last - 1, 1, 0, SUPER, "ssss", False)
+        evacuate(last - 1, 1, 0, SUPER, "ssss", True)
         new_block(last, 1)
         combine(last, 1, pieces[:1])
         quantise(last, 0, 0, SUPER)
         multiply(last, 0, 0, SUPER)
-        evacuate(last, 0, 0, SUPER, "ssss", False)
+        evacuate(last, 0, 0, SUPER, "ssss", True)
         for i, (dst0, src0, n) in enumerate(pieces):
             if i + 1 < len(pieces):
                 combine(last, 1, pieces[i + 1 : i + 2])
             quantise(last, 1, dst0, n)
             multiply(last, 1, dst0, n)
         for i, (dst0, src0, n) in enumerate(pieces):
-            evacuate(last, 1, dst0, n, "svsv", i + 1 == len(pieces))
+            evacuate(last, 1, dst0, n, "svsv", True)

@@ -167,9 +167,9 @@ def tile_dlrkernel_t_kernel(tc, W, Lambda_im, L, out):
             grouped = grouped_tiles[(m, s)]
             for dst0, src0, n in spans:
                 nc.vector.tensor_tensor(
-                    out=grouped[:, dst0 : dst0 + n, :].rearrange("p (c i) t -> p c t i", i=4),
-                    in0=u_tiles[m][:, :, src0 : src0 + n].rearrange("p t (c i) -> p c t i", i=4),
-                    in1=v_tiles[m][:, :, src0 : src0 + n].rearrange("p t (c i) -> p c t i", i=4),
+                    out=grouped[:, dst0 : dst0 + n, :].rearrange("p (c i) t -> p c t i", i=8),
+                    in0=u_tiles[m][:, :, src0 : src0 + n].rearrange("p t (c i) -> p c t i", i=8),
+                    in1=v_tiles[m][:, :, src0 : src0 + n].rearrange("p t (c i) -> p c t i", i=8),
                     op=ALU.subtract if s == 0 else ALU.add,
                 )
 

@@ -46,6 +46,7 @@ def tile_dlrkernel_t_kernel(tc, W, Lambda_im, L, out):
         lam_bf = const.tile([P, PACK], BF16)
         nc.sync.dma_start(out=lam_bf[:], in_=Lambda_im.rearrange("(p t) -> p t", t=PACK))
         w_sb = const.tile([P, h_tiles, N], BF16)
+        nc.gpsimd.tensor_copy(out=w_sb[:, 0, 0:PACK], in_=lam_bf[:])
         nc.sync.dma_start(out=w_sb[:], in_=W[0].rearrange("(a p) n -> p a n", p=P))
 
         warm = const.tile([P, 1], F32)

@@ -18,7 +18,7 @@ BLOCK = 256
 SUPER = 512
 T_GROUP = 1
 FIRST_V_ON_VECTOR = 2
-U_ON_SCALAR = 1
+U_ON_SCALAR = 0
 
 FLOPS = 2 * 512 * 512 * 8192
 

@@ -19,6 +19,7 @@ SUPER = 512
 T_GROUP = 1
 FIRST_V_ON_VECTOR = 2
 U_ON_SCALAR = 0
+U_ON_SCALAR_LAST = 4
 
 FLOPS = 2 * 512 * 512 * 8192
 
@@ -220,7 +221,8 @@ def tile_dlrkernel_t_kernel(tc, W, Lambda_im, L, out):
             if m > 0:
                 evacuate(m - 1, 1, 0, SUPER, "ssss", False)
             new_products(m + 1)
-            first = todo[U_ON_SCALAR:cut]
+            u_s = U_ON_SCALAR_LAST if m + 1 == last else U_ON_SCALAR
+            first = todo[u_s:cut]
             if m == 0:
                 w_quantise()
                 first = []
@@ -228,14 +230,14 @@ def tile_dlrkernel_t_kernel(tc, W, Lambda_im, L, out):
                 product(m + 1, r, t, 0, "v")
             quantise(m, 0, 0, SUPER)
             multiply(m, 0, 0, SUPER)
-            for r, t in todo[:U_ON_SCALAR]:
+            for r, t in todo[:u_s]:
                 product(m + 1, r, t, 0, "s")
             for r, t in todo:
                 product(m + 1, r, t, 1, "s")
             new_block(m, 1)
             combine(m, 1, spans_of(1))
             if m == 0:
-                for r, t in todo[U_ON_SCALAR:cut]:
+                for r, t in todo[u_s:cut]:
                     product(m + 1, r, t, 0, "v")
             for r, t in todo[cut:]:
                 product(m + 1, r, t, 0, "v")

@@ -259,5 +259,13 @@ def tile_dlrkernel_t_kernel(tc, W, Lambda_im, L, out):
                 combine(last, 1, pieces[i + 1 : i + 2])
             quantise(last, 1, dst0, n)
             multiply(last, 1, dst0, n)
+        low = L // 2 - SUPER * (last + 1)
+        stage = work.tile([P, h_tiles, SUPER], F32, name="stage", tag="stage", bufs=4)
         for i, (dst0, src0, n) in enumerate(pieces):
-            evacuate(last, 1, dst0, n, "svsv", True)
+            for a in range(h_tiles):
+                if a % 2 == 1:
+                    nc.vector.tensor_copy(out=stage[:, a, dst0 : dst0 + n], in_=acc_tiles[(last, 1, dst0)][a][:])
+                else:
+                    nc.scalar.copy(out=stage[:, a, dst0 : dst0 + n], in_=acc_tiles[(last, 1, dst0)][a][:])
+                if i + 1 == len(pieces):
+                    nc.sync.dma_start(out=out_view[:, a, low : low + SUPER], in_=stage[:, a, :])

@@ -20,6 +20,7 @@ T_GROUP = 1
 FIRST_V_ON_VECTOR = 2
 U_ON_SCALAR = 0
 U_ON_SCALAR_LAST = 4
+ANGLES_ON_SCALAR = 2
 
 FLOPS = 2 * 512 * 512 * 8192
 
@@ -69,6 +70,8 @@ def tile_dlrkernel_t_kernel(tc, W, Lambda_im, L, out):
         make_identity(nc, ident[:])
 
         lam = lam_bf
+        lam_f32 = const.tile([P, PACK], F32)
+        nc.scalar.copy(out=lam_f32[:], in_=lam_bf[:])
         turns = const.tile([P, PACK], F32)
         nc.vector.tensor_scalar(out=turns[:], in0=lam[:], scalar1=1.0 / (2.0 * math.pi), scalar2=None, op0=ALU.mult)
 
@@ -133,7 +136,10 @@ def tile_dlrkernel_t_kernel(tc, W, Lambda_im, L, out):
                 nc.vector.tensor_scalar(
                     out=k_int[:, t, :], in0=pos[:], scalar1=turns[:, t : t + 1], scalar2=ROUND_SHIFT, op0=ALU.mult, op1=ALU.add
                 )
-                nc.vector.tensor_scalar(out=angle[:, t, :], in0=pos[:], scalar1=lam[:, t : t + 1], scalar2=None, op0=ALU.mult)
+                if t < ANGLES_ON_SCALAR:
+                    nc.scalar.activation(out=angle[:, t, :], in_=pos[:], func=ACT.Copy, scale=lam_f32[:, t : t + 1])
+                else:
+                    nc.vector.tensor_scalar(out=angle[:, t, :], in0=pos[:], scalar1=lam[:, t : t + 1], scalar2=None, op0=ALU.mult)
             nc.vector.scalar_tensor_tensor(
                 out=part[:, lo:hi, :], in0=k_int[:, lo:hi, :], scalar=-TWO_PI_HI, in1=angle[:, lo:hi, :], op0=ALU.mult, op1=ALU.add
             )

@@ -20,7 +20,7 @@ T_GROUP = 1
 FIRST_V_ON_VECTOR = 2
 U_ON_SCALAR = 0
 U_ON_SCALAR_LAST = 4
-ANGLES_ON_SCALAR = 2
+ANGLES_ON_SCALAR = 4
 
 FLOPS = 2 * 512 * 512 * 8192
 

import math

import concourse.mybir as mybir
from concourse.masks import make_identity

F32 = mybir.dt.float32
BF16 = mybir.dt.bfloat16
I32 = mybir.dt.int32
U32 = mybir.dt.uint32
U8 = mybir.dt.uint8
FP8X4 = mybir.dt.float8_e4m3fn_x4
ALU = mybir.AluOpType
ACT = mybir.ActivationFunctionType

P = 128
PACK = 4
BLOCK = 256
SUPER = 512
T_GROUP = 1
FIRST_V_ON_VECTOR = 2
U_ON_SCALAR = 0
U_ON_SCALAR_LAST = 4
ANGLES_ON_SCALAR = 4

FLOPS = 2 * 512 * 512 * 8192

TWO_PI_HI = 3217.0 / 512.0
TWO_PI_LO = 2.0 * math.pi - TWO_PI_HI
ROUND_SHIFT = -0.125


def tile_dlrkernel_t_kernel(tc, W, Lambda_im, L, out):
    nc = tc.nc
    H = W.shape[1]
    N = W.shape[2]
    assert N == P * PACK and H % (2 * P) == 0 and L % (2 * SUPER) == 0
    h_tiles = H // P
    subs = SUPER // BLOCK
    pairs = L // (2 * BLOCK)
    supers = L // (2 * SUPER)
    centre = (L - BLOCK) // 2
    width = BLOCK + pairs
    out_view = out[0].rearrange("(a p) l -> p a l", p=P)

    with tc.tile_pool(name="const", bufs=1) as const, tc.tile_pool(name="work", bufs=3) as work, tc.psum_pool(
        name="psum", bufs=8
    ) as psum:
        lam_bf = const.tile([P, PACK], BF16)
        nc.sync.dma_start(out=lam_bf[:], in_=Lambda_im.rearrange("(p t) -> p t", t=PACK))
        w_sb = const.tile([P, h_tiles, N], BF16)
        nc.gpsimd.tensor_copy(out=w_sb[:, 0, 0:PACK], in_=lam_bf[:])
        nc.sync.dma_start(out=w_sb[:], in_=W[0].rearrange("(a p) n -> p a n", p=P))

        warm = const.tile([P, 1], F32)
        nc.vector.memset(warm[:], 0.0)
        nc.scalar.activation(out=warm[:], in_=warm[:], func=ACT.Sin)

        pos = const.tile([P, width], F32)
        nc.gpsimd.iota(
            pos[:, 0:BLOCK], pattern=[[1, BLOCK]], base=centre, channel_multiplier=0, allow_small_or_imprecise_dtypes=True
        )
        nc.gpsimd.iota(
            pos[:, BLOCK:width],
            pattern=[[BLOCK, pairs]],
            base=BLOCK // 2,
            channel_multiplier=0,
            allow_small_or_imprecise_dtypes=True,
        )
        ident = const.tile([P, P], F32)
        make_identity(nc, ident[:])

        lam = lam_bf
        lam_f32 = const.tile([P, PACK], F32)
        nc.scalar.copy(out=lam_f32[:], in_=lam_bf[:])
        turns = const.tile([P, PACK], F32)
        nc.vector.tensor_scalar(out=turns[:], in0=lam[:], scalar1=1.0 / (2.0 * math.pi), scalar2=None, op0=ALU.mult)

        w_grouped = const.tile([P, H, 2], F32, align_bytes=64)
        w_codes = const.tile([P, H], U32, align_bytes=64)
        w_scales = const.tile([P, H], U8, align_bytes=64)
        turned_tiles = []
        for half in range(h_tiles // 2):
            turned = psum.tile([P, 2, 2, P], F32, name="turned", tag="acc")
            turned_tiles.append(turned)
            for a in range(2):
                words = w_sb[:, 2 * half + a, :].bitcast(F32).rearrange("p (q u) -> p u q", u=2)
                for u in range(2):
                    nc.tensor.transpose(turned[:, a, u, :], words[:, u, :], ident[:])

        def w_copies():
            for half in range(h_tiles // 2):
                nc.scalar.copy(
                    out=w_grouped[:, 2 * P * half : 2 * P * (half + 1), :].rearrange("p (a h) u -> p a h u", a=2),
                    in_=turned_tiles[half][:].rearrange("p a u h -> p a h u"),
                )

        def w_quantise():
            nc.vector.quantize_mx(
                out=w_codes[:].bitcast(FP8X4),
                scales=w_scales[:],
                in_=w_grouped[:].rearrange("p h u -> p (h u)").bitcast(BF16),
            )

        table = const.tile([P, PACK, 2, width], F32)
        k_int = const.tile([P, PACK, width], I32)
        angle = const.tile([P, PACK, width], F32)
        part = const.tile([P, PACK, width], F32)
        red = const.tile([P, PACK, width], F32)
        fold = const.tile([P, PACK, 2, width], F32)

        u_tiles = {}
        v_tiles = {}

        def product_list(m):
            return [(r, t) for t in range(PACK) for r in range(subs)]

        def new_products(m):
            u_tiles[m] = work.tile([P, PACK, SUPER], F32, name="u_t", tag="u_t")
            v_tiles[m] = work.tile([P, PACK, SUPER], F32, name="v_t", tag="v_t")

        def product(m, r, t, which, engine):
            k = subs * m + r
            dst = (u_tiles[m] if which == 0 else v_tiles[m])[:, t, r * BLOCK : (r + 1) * BLOCK]
            src = table[:, t, which, 0:BLOCK]
            factor = table[:, t, which, BLOCK + k : BLOCK + k + 1]
            if engine == "v":
                nc.vector.tensor_scalar(out=dst, in0=src, scalar1=factor, scalar2=None, op0=ALU.mult)
            else:
                nc.scalar.activation(out=dst, in_=src, func=ACT.Copy, scale=factor)

        new_products(0)
        groups = [list(range(g, g + T_GROUP)) for g in range(0, PACK, T_GROUP)]
        for gi, ts in enumerate(groups):
            lo, hi = ts[0], ts[-1] + 1
            for t in ts:
                nc.vector.tensor_scalar(
                    out=k_int[:, t, :], in0=pos[:], scalar1=turns[:, t : t + 1], scalar2=ROUND_SHIFT, op0=ALU.mult, op1=ALU.add
                )
                if t < ANGLES_ON_SCALAR:
                    nc.scalar.activation(out=angle[:, t, :], in_=pos[:], func=ACT.Copy, scale=lam_f32[:, t : t + 1])
                else:
                    nc.vector.tensor_scalar(out=angle[:, t, :], in0=pos[:], scalar1=lam[:, t : t + 1], scalar2=None, op0=ALU.mult)
            nc.vector.scalar_tensor_tensor(
                out=part[:, lo:hi, :], in0=k_int[:, lo:hi, :], scalar=-TWO_PI_HI, in1=angle[:, lo:hi, :], op0=ALU.mult, op1=ALU.add
            )
            nc.vector.scalar_tensor_tensor(
                out=red[:, lo:hi, :], in0=k_int[:, lo:hi, :], scalar=-TWO_PI_LO, in1=part[:, lo:hi, :], op0=ALU.mult, op1=ALU.add
            )
            nc.scalar.activation(out=fold[:, lo:hi, 0, :], in_=red[:, lo:hi, :], func=ACT.Abs)
            nc.scalar.activation(out=fold[:, lo:hi, 1, :], in_=red[:, lo:hi, :], func=ACT.Abs, bias=-0.5 * math.pi)
            nc.scalar.activation(
                out=table[:, lo:hi, :, :], in_=fold[:, lo:hi, :, :], func=ACT.Sin, scale=-1.0, bias=0.5 * math.pi
            )
        for r, t in product_list(0):
            product(0, r, t, 0, "v")
            product(0, r, t, 1, "v" if t < FIRST_V_ON_VECTOR else "s")
        w_copies()

        grouped_tiles = {}
        code_tiles = {}
        acc_tiles = {}

        def spans_of(s):
            if s == 0:
                return [(0, 0, SUPER)]
            return [((subs - 1 - r) * BLOCK, r * BLOCK, BLOCK) for r in range(subs)]

        def new_block(m, s):
            grouped_tiles[(m, s)] = work.tile([P, SUPER, PACK], BF16, name="grouped", tag="grouped", align_bytes=64)
            codes = work.tile([P, SUPER], U32, name="codes", tag="codes", align_bytes=64)
            scales = work.tile([P, SUPER], U8, name="scales", tag="scales", align_bytes=64)
            code_tiles[(m, s)] = (codes, scales)

        def combine(m, s, spans):
            grouped = grouped_tiles[(m, s)]
            for dst0, src0, n in spans:
                nc.vector.tensor_tensor(
                    out=grouped[:, dst0 : dst0 + n, :].rearrange("p (c i) t -> p c t i", i=8),
                    in0=u_tiles[m][:, :, src0 : src0 + n].rearrange("p t (c i) -> p c t i", i=8),
                    in1=v_tiles[m][:, :, src0 : src0 + n].rearrange("p t (c i) -> p c t i", i=8),
                    op=ALU.subtract if s == 0 else ALU.add,
                )

        def quantise(m, s, c0, n):
            codes, scales = code_tiles[(m, s)]
            nc.vector.quantize_mx(
                out=codes[:, c0 : c0 + n].bitcast(FP8X4),
                scales=scales[:, c0 : c0 + n],
                in_=grouped_tiles[(m, s)][:, c0 : c0 + n, :].rearrange("p l t -> p (l t)"),
            )

        def multiply(m, s, c0, n):
            codes, scales = code_tiles[(m, s)]
            acc_tiles[(m, s, c0)] = []
            for a in range(h_tiles):
                acc = psum.tile([P, n], F32, name="acc", tag="acc")
                acc_tiles[(m, s, c0)].append(acc)
                nc.tensor.matmul_mx(
                    out=acc[:],
                    lhsT=w_codes[:, a * P : (a + 1) * P].bitcast(FP8X4),
                    lhsT_scale=w_scales[:, a * P : (a + 1) * P],
                    rhs=codes[:, c0 : c0 + n].bitcast(FP8X4),
                    rhs_scale=scales[:, c0 : c0 + n],
                    start=True,
                    stop=True,
                )

        def evacuate(m, s, c0, n, engines, split):
            start = (L // 2 + SUPER * m if s == 0 else L // 2 - SUPER * (m + 1)) + c0
            stage = work.tile([P, h_tiles, n], F32, name="stage", tag="stage", bufs=4)
            for a in range(h_tiles):
                if engines[a] == "v":
                    nc.vector.tensor_copy(out=stage[:, a, :], in_=acc_tiles[(m, s, c0)][a][:])
                else:
                    nc.scalar.copy(out=stage[:, a, :], in_=acc_tiles[(m, s, c0)][a][:])
                if split:
                    nc.sync.dma_start(out=out_view[:, a, start : start + n], in_=stage[:, a, :])
            if not split:
                nc.sync.dma_start(out=out_view[:, :, start : start + n], in_=stage[:])

        last = supers - 1
        for m in range(last):
            todo = product_list(m + 1)
            cut = len(todo) // 2
            new_block(m, 0)
            combine(m, 0, spans_of(0))
            if m > 0:
                evacuate(m - 1, 1, 0, SUPER, "ssss", False)
            new_products(m + 1)
            u_s = U_ON_SCALAR_LAST if m + 1 == last else U_ON_SCALAR
            first = todo[u_s:cut]
            if m == 0:
                w_quantise()
                first = []
            for r, t in first:
                product(m + 1, r, t, 0, "v")
            quantise(m, 0, 0, SUPER)
            multiply(m, 0, 0, SUPER)
            for r, t in todo[:u_s]:
                product(m + 1, r, t, 0, "s")
            for r, t in todo:
                product(m + 1, r, t, 1, "s")
            new_block(m, 1)
            combine(m, 1, spans_of(1))
            if m == 0:
                for r, t in todo[u_s:cut]:
                    product(m + 1, r, t, 0, "v")
            for r, t in todo[cut:]:
                product(m + 1, r, t, 0, "v")
            quantise(m, 1, 0, SUPER)
            multiply(m, 1, 0, SUPER)
            evacuate(m, 0, 0, SUPER, "ssss", False)

        pieces = spans_of(1)
        new_block(last, 0)
        combine(last, 0, spans_of(0))
        evacuate(last - 1, 1, 0, SUPER, "ssss", True)
        new_block(last, 1)
        combine(last, 1, pieces[:1])
        quantise(last, 0, 0, SUPER)
        multiply(last, 0, 0, SUPER)
        evacuate(last, 0, 0, SUPER, "ssss", True)
        for i, (dst0, src0, n) in enumerate(pieces):
            if i + 1 < len(pieces):
                combine(last, 1, pieces[i + 1 : i + 2])
            quantise(last, 1, dst0, n)
            multiply(last, 1, dst0, n)
        low = L // 2 - SUPER * (last + 1)
        stage = work.tile([P, h_tiles, SUPER], F32, name="stage", tag="stage", bufs=4)
        for i, (dst0, src0, n) in enumerate(pieces):
            for a in range(h_tiles):
                if a % 2 == 1:
                    nc.vector.tensor_copy(out=stage[:, a, dst0 : dst0 + n], in_=acc_tiles[(last, 1, dst0)][a][:])
                else:
                    nc.scalar.copy(out=stage[:, a, dst0 : dst0 + n], in_=acc_tiles[(last, 1, dst0)][a][:])
                if i + 1 == len(pieces):
                    nc.sync.dma_start(out=out_view[:, a, low : low + SUPER], in_=stage[:, a, :])
